import numpy as np
import ml_dtypes


def mxq(x, axis, fmt="e4m3"):
    dtype, down = {"e4m3": (ml_dtypes.float8_e4m3fn, 7), "e5m2": (ml_dtypes.float8_e5m2, 14)}[fmt]
    v = np.moveaxis(np.asarray(x, np.float32).astype(ml_dtypes.bfloat16).astype(np.float64), axis, -1)
    blocks = v.reshape(v.shape[:-1] + (-1, 32))
    amax = np.abs(blocks).max(-1, keepdims=True)
    byte = np.maximum(np.where(amax > 0, np.frexp(amax)[1] - 1 + 127, 0) - down, 1)
    scale = np.exp2(byte - 127.0)
    codes = (blocks / scale).astype(np.float32).astype(dtype).astype(np.float64)
    return np.moveaxis((codes * scale).reshape(v.shape), -1, axis)


WIDE = False


def mx_kscale(k):
    if not WIDE:
        return np.ones(k)
    levels = np.array([10, -10, 5, -5, 0])
    a = np.random.permutation(np.resize(levels, k // 512 * 4)).reshape(k // 512, 4)
    idx = np.arange(k)
    return np.exp2(a[idx // 512, idx % 128 // 32])


BF16 = ml_dtypes.bfloat16


def bf(x):
    return np.asarray(x, np.float32).astype(BF16)


def f64(x):
    return np.asarray(x).astype(np.float64)


U, I, D = 8192, 256, 512
C = 1.0
EPS = 1e-7
MAX_SQDIST = 50.0


def setup_inputs():
    s = mx_kscale(D)
    a = np.sqrt(600.0 / np.sqrt(D))
    hu = np.random.standard_normal((U, D)) * a * s
    hi = np.random.standard_normal((I, D)) * a / s
    return {"h": bf(np.concatenate([hu, hi], 0))}


def reference(h):
    h = f64(h)
    hu = h[:U]
    hi = h[U:U + I]
    signs = np.concatenate([-np.ones(1), np.ones(D - 1)])
    prod = mxq(hu, 1, "e4m3") @ mxq(hi * signs, 1, "e4m3").T
    K = 1.0 / C
    theta = np.maximum(-prod / K, 1.0 + EPS)
    sqdist = np.minimum(K * np.arccosh(theta) ** 2, MAX_SQDIST)
    return -sqdist

@@ -1,0 +1,173 @@
+import math
+from contextlib import ExitStack
+
+import concourse.mybir as mybir
+from concourse.masks import make_identity
+
+F32 = mybir.dt.float32
+BF16 = mybir.dt.bfloat16
+U32 = mybir.dt.uint32
+U8 = mybir.dt.uint8
+FP8X4 = mybir.dt.float8_e4m3fn_x4
+ALU = mybir.AluOpType
+ACT = mybir.ActivationFunctionType
+
+P = 128
+USERS, ITEMS, COORDS = 8192, 256, 512
+FLOPS = 2 * USERS * ITEMS * COORDS
+
+WORDS = COORDS // 2
+HALVES = WORDS // P
+USER_TILES = USERS // P
+ITEM_TILES = ITEMS // P
+TILES_PER_BANK = 2
+BANKS_PER_GROUP = 2
+GROUP = TILES_PER_BANK * BANKS_PER_GROUP
+N_GROUPS = USER_TILES // GROUP
+GROUP_COLS = GROUP * ITEMS
+
+THETA_MIN = 1.0 + 1e-7
+MAX_SQDIST = 50.0
+THETA_MAX = 0.5 * (math.exp(math.sqrt(MAX_SQDIST)) + math.exp(-math.sqrt(MAX_SQDIST)))
+
+
+def tile_hgatmodel_t_kernel(tc, h, out):
+    nc = tc.nc
+    users_in = h[0:USERS, :].rearrange("(p t) d -> p (t d)", t=USER_TILES)
+    items_in = h[USERS : USERS + ITEMS, :].rearrange("(j p) d -> p j d", p=P)
+    result_out = out.rearrange("(p t) i -> p (t i)", t=USER_TILES)
+
+    with ExitStack() as ctx:
+        consts = ctx.enter_context(tc.tile_pool(name="consts", bufs=1))
+        rows = ctx.enter_context(tc.tile_pool(name="rows", bufs=N_GROUPS))
+        stage = ctx.enter_context(tc.tile_pool(name="stage", bufs=3))
+        thetas = ctx.enter_context(tc.tile_pool(name="thetas", bufs=4))
+        results = ctx.enter_context(tc.tile_pool(name="results", bufs=N_GROUPS))
+        flipped = ctx.enter_context(tc.psum_pool(name="flipped", bufs=4))
+        products = ctx.enter_context(tc.psum_pool(name="products", bufs=4))
+        ctx.enter_context(tc.manual_schedule())
+
+        item_rows = consts.tile([P, ITEM_TILES * COORDS], BF16)
+        nc.sync.dma_start(out=item_rows[:].rearrange("p (j d) -> p j d", j=ITEM_TILES), in_=items_in)
+        user_rows = {}
+        for g in range(N_GROUPS):
+            user_rows[g] = rows.tile([P, GROUP * COORDS], BF16, name="user_rows")
+            nc.sync.dma_start(
+                out=user_rows[g][:], in_=users_in[:, g * GROUP * COORDS : (g + 1) * GROUP * COORDS]
+            )
+
+        identity = consts.tile([P, P], F32)
+        make_identity(nc, identity[:])
+        minus_one = consts.tile([P, 1], F32)
+        nc.vector.memset(minus_one[:], -1.0)
+        table_warmer = consts.tile([P, 1], F32)
+        nc.scalar.activation(out=table_warmer[:], in_=minus_one[:], func=ACT.Sqrt, scale=-1.0)
+
+        def transpose_tiles(source, n_tiles):
+            words = source[:].bitcast(F32)
+            banks = []
+            for b in range(n_tiles // TILES_PER_BANK):
+                bank = flipped.tile([P, TILES_PER_BANK, HALVES, P], F32, name="bank")
+                for t in range(TILES_PER_BANK):
+                    for u in range(HALVES):
+                        first = ((b * TILES_PER_BANK + t) * HALVES + u) * P
+                        nc.tensor.transpose(bank[:, t, u, :], words[:, first : first + P], identity[:])
+                banks.append(bank)
+            return banks
+
+        def regroup(copy, bank, grouped, b):
+            as_words = grouped[:].bitcast(F32).rearrange("p (t r u) -> p t r u", r=P, u=HALVES)
+            copy(
+                out=as_words[:, b * TILES_PER_BANK : (b + 1) * TILES_PER_BANK],
+                in_=bank[:].rearrange("p t u r -> p t r u"),
+            )
+
+        def quantise(pool, grouped, n_tiles):
+            codes = pool.tile([P, n_tiles * P], U32, name="codes%d" % n_tiles, align_bytes=64)
+            scales = pool.tile([P, n_tiles * P], U8, name="scales%d" % n_tiles, align_bytes=64)
+            nc.vector.quantize_mx(out=codes[:].bitcast(FP8X4), scales=scales[:], in_=grouped[:])
+            return codes, scales
+
+        first_coord = item_rows[:].rearrange("p (j d) -> p j d", j=ITEM_TILES)[:, :, 0:1]
+        nc.vector.tensor_scalar(out=first_coord, in0=first_coord, scalar1=-1.0, scalar2=None, op0=ALU.mult)
+        item_banks = transpose_tiles(item_rows, ITEM_TILES)
+        item_grouped = consts.tile([P, ITEM_TILES * COORDS], BF16, align_bytes=64)
+        regroup(nc.vector.tensor_copy, item_banks[0], item_grouped, 0)
+        item_codes, item_scales = quantise(consts, item_grouped, ITEM_TILES)
+
+        banks_of, grouped_of, quantised_of, product_of, theta_of, work_of = {}, {}, {}, {}, {}, {}
+
+        def transpose_users(g):
+            banks_of[g] = transpose_tiles(user_rows[g], GROUP)
+
+        def regroup_users(g):
+            grouped_of[g] = stage.tile([P, GROUP * COORDS], BF16, name="grouped", align_bytes=64)
+            for b in range(BANKS_PER_GROUP):
+                on_vector = (g * BANKS_PER_GROUP + b) % 4 == 3
+                regroup(nc.vector.tensor_copy if on_vector else nc.scalar.copy, banks_of[g][b], grouped_of[g], b)
+
+        def quantise_users(g):
+            quantised_of[g] = quantise(stage, grouped_of[g], GROUP)
+
+        def multiply(g):
+            codes, scales = quantised_of[g]
+            product_of[g] = []
+            for b in range(BANKS_PER_GROUP):
+                bank = products.tile([P, TILES_PER_BANK, ITEMS], F32, name="product")
+                for t in range(TILES_PER_BANK):
+                    cols = slice((b * TILES_PER_BANK + t) * P, (b * TILES_PER_BANK + t + 1) * P)
+                    nc.tensor.matmul_mx(
+                        out=bank[:, t, :],
+                        lhsT=codes[:, cols].bitcast(FP8X4),
+                        lhsT_scale=scales[:, cols],
+                        rhs=item_codes[:].bitcast(FP8X4),
+                        rhs_scale=item_scales[:],
+                        start=True,
+                        stop=True,
+                    )
+                product_of[g].append(bank)
+
+        def clamp(g):
+            theta_of[g] = thetas.tile([P, GROUP_COLS], F32, name="minus_theta")
+            width = TILES_PER_BANK * ITEMS
+            for b in range(BANKS_PER_GROUP):
+                nc.vector.tensor_scalar(
+                    out=theta_of[g][:, b * width : (b + 1) * width],
+                    in0=product_of[g][b][:].rearrange("p t i -> p (t i)"),
+                    scalar1=-THETA_MIN,
+                    scalar2=-THETA_MAX,
+                    op0=ALU.min,
+                    op1=ALU.max,
+                )
+
+        def square(g):
+            work_of[g] = results.tile([P, GROUP_COLS], F32, name="work")
+            nc.scalar.activation(out=work_of[g][:], in_=theta_of[g][:], func=ACT.Square)
+
+        def root(g):
+            nc.scalar.activation(out=work_of[g][:], in_=work_of[g][:], func=ACT.Sqrt, bias=minus_one[:], scale=1.0)
+
+        def add_theta(g):
+            nc.vector.tensor_tensor(out=work_of[g][:], in0=work_of[g][:], in1=theta_of[g][:], op=ALU.subtract)
+
+        def run(stage_fn, g):
+            if 0 <= g < N_GROUPS:
+                stage_fn(g)
+
+        LAST_LAG = 6
+        for step in range(N_GROUPS + LAST_LAG):
+            run(transpose_users, step)
+            run(regroup_users, step - 1)
+            run(quantise_users, step - 2)
+            run(multiply, step - 2)
+            run(clamp, step - 3)
+            run(square, step - 4)
+            run(root, step - 5)
+            run(add_theta, step - LAST_LAG)
+
+        for g in range(N_GROUPS):
+            nc.scalar.activation(out=work_of[g][:], in_=work_of[g][:], func=ACT.Ln)
+            nc.vector.scalar_tensor_tensor(
+                out=work_of[g][:], in0=work_of[g][:], scalar=-1.0, in1=work_of[g][:], op0=ALU.mult, op1=ALU.mult
+            )
+            nc.sync.dma_start(out=result_out[:, g * GROUP_COLS : (g + 1) * GROUP_COLS], in_=work_of[g][:])

@@ -25,6 +25,7 @@ BANKS_PER_GROUP = 2
 GROUP = TILES_PER_BANK * BANKS_PER_GROUP
 N_GROUPS = USER_TILES // GROUP
 GROUP_COLS = GROUP * ITEMS
+GPSIMD_COLS = 3 * ITEMS
 
 THETA_MIN = 1.0 + 1e-7
 MAX_SQDIST = 50.0
@@ -41,7 +42,7 @@ def tile_hgatmodel_t_kernel(tc, h, out):
         consts = ctx.enter_context(tc.tile_pool(name="consts", bufs=1))
         rows = ctx.enter_context(tc.tile_pool(name="rows", bufs=N_GROUPS))
         stage = ctx.enter_context(tc.tile_pool(name="stage", bufs=3))
-        thetas = ctx.enter_context(tc.tile_pool(name="thetas", bufs=4))
+        thetas = ctx.enter_context(tc.tile_pool(name="thetas", bufs=6))
         results = ctx.enter_context(tc.tile_pool(name="results", bufs=N_GROUPS))
         flipped = ctx.enter_context(tc.psum_pool(name="flipped", bufs=4))
         products = ctx.enter_context(tc.psum_pool(name="products", bufs=4))
@@ -103,7 +104,7 @@ def tile_hgatmodel_t_kernel(tc, h, out):
         def regroup_users(g):
             grouped_of[g] = stage.tile([P, GROUP * COORDS], BF16, name="grouped", align_bytes=64)
             for b in range(BANKS_PER_GROUP):
-                on_vector = (g * BANKS_PER_GROUP + b) % 4 == 3
+                on_vector = b == 1
                 regroup(nc.vector.tensor_copy if on_vector else nc.scalar.copy, banks_of[g][b], grouped_of[g], b)
 
         def quantise_users(g):
@@ -148,7 +149,10 @@ def tile_hgatmodel_t_kernel(tc, h, out):
             nc.scalar.activation(out=work_of[g][:], in_=work_of[g][:], func=ACT.Sqrt, bias=minus_one[:], scale=1.0)
 
         def add_theta(g):
-            nc.vector.tensor_tensor(out=work_of[g][:], in0=work_of[g][:], in1=theta_of[g][:], op=ALU.subtract)
+            for engine, cols in ((nc.gpsimd, slice(0, GPSIMD_COLS)), (nc.vector, slice(GPSIMD_COLS, GROUP_COLS))):
+                engine.tensor_tensor(
+                    out=work_of[g][:, cols], in0=work_of[g][:, cols], in1=theta_of[g][:, cols], op=ALU.subtract
+                )
 
         def run(stage_fn, g):
             if 0 <= g < N_GROUPS:
@@ -157,13 +161,13 @@ def tile_hgatmodel_t_kernel(tc, h, out):
         LAST_LAG = 6
         for step in range(N_GROUPS + LAST_LAG):
             run(transpose_users, step)
-            run(regroup_users, step - 1)
             run(quantise_users, step - 2)
+            run(add_theta, step - LAST_LAG)
             run(multiply, step - 2)
             run(clamp, step - 3)
+            run(regroup_users, step - 1)
             run(square, step - 4)
             run(root, step - 5)
-            run(add_theta, step - LAST_LAG)
 
         for g in range(N_GROUPS):
             nc.scalar.activation(out=work_of[g][:], in_=work_of[g][:], func=ACT.Ln)

@@ -25,7 +25,6 @@ BANKS_PER_GROUP = 2
 GROUP = TILES_PER_BANK * BANKS_PER_GROUP
 N_GROUPS = USER_TILES // GROUP
 GROUP_COLS = GROUP * ITEMS
-GPSIMD_COLS = 3 * ITEMS
 
 THETA_MIN = 1.0 + 1e-7
 MAX_SQDIST = 50.0
@@ -104,7 +103,7 @@ def tile_hgatmodel_t_kernel(tc, h, out):
         def regroup_users(g):
             grouped_of[g] = stage.tile([P, GROUP * COORDS], BF16, name="grouped", align_bytes=64)
             for b in range(BANKS_PER_GROUP):
-                on_vector = b == 1
+                on_vector = (g * BANKS_PER_GROUP + b) % 4 == 3
                 regroup(nc.vector.tensor_copy if on_vector else nc.scalar.copy, banks_of[g][b], grouped_of[g], b)
 
         def quantise_users(g):
@@ -149,25 +148,22 @@ def tile_hgatmodel_t_kernel(tc, h, out):
             nc.scalar.activation(out=work_of[g][:], in_=work_of[g][:], func=ACT.Sqrt, bias=minus_one[:], scale=1.0)
 
         def add_theta(g):
-            for engine, cols in ((nc.gpsimd, slice(0, GPSIMD_COLS)), (nc.vector, slice(GPSIMD_COLS, GROUP_COLS))):
-                engine.tensor_tensor(
-                    out=work_of[g][:, cols], in0=work_of[g][:, cols], in1=theta_of[g][:, cols], op=ALU.subtract
-                )
+            nc.vector.tensor_tensor(out=work_of[g][:], in0=work_of[g][:], in1=theta_of[g][:], op=ALU.subtract)
 
         def run(stage_fn, g):
             if 0 <= g < N_GROUPS:
                 stage_fn(g)
 
-        LAST_LAG = 6
+        LAST_LAG = 7
         for step in range(N_GROUPS + LAST_LAG):
             run(transpose_users, step)
             run(quantise_users, step - 2)
-            run(add_theta, step - LAST_LAG)
             run(multiply, step - 2)
             run(clamp, step - 3)
             run(regroup_users, step - 1)
             run(square, step - 4)
             run(root, step - 5)
+            run(add_theta, step - LAST_LAG)
 
         for g in range(N_GROUPS):
             nc.scalar.activation(out=work_of[g][:], in_=work_of[g][:], func=ACT.Ln)

import math
from contextlib import ExitStack

import concourse.mybir as mybir
from concourse.masks import make_identity

F32 = mybir.dt.float32
BF16 = mybir.dt.bfloat16
U32 = mybir.dt.uint32
U8 = mybir.dt.uint8
FP8X4 = mybir.dt.float8_e4m3fn_x4
ALU = mybir.AluOpType
ACT = mybir.ActivationFunctionType

P = 128
USERS, ITEMS, COORDS = 8192, 256, 512
FLOPS = 2 * USERS * ITEMS * COORDS

WORDS = COORDS // 2
HALVES = WORDS // P
USER_TILES = USERS // P
ITEM_TILES = ITEMS // P
TILES_PER_BANK = 2
BANKS_PER_GROUP = 2
GROUP = TILES_PER_BANK * BANKS_PER_GROUP
N_GROUPS = USER_TILES // GROUP
GROUP_COLS = GROUP * ITEMS

THETA_MIN = 1.0 + 1e-7
MAX_SQDIST = 50.0
THETA_MAX = 0.5 * (math.exp(math.sqrt(MAX_SQDIST)) + math.exp(-math.sqrt(MAX_SQDIST)))


def tile_hgatmodel_t_kernel(tc, h, out):
    nc = tc.nc
    users_in = h[0:USERS, :].rearrange("(p t) d -> p (t d)", t=USER_TILES)
    items_in = h[USERS : USERS + ITEMS, :].rearrange("(j p) d -> p j d", p=P)
    result_out = out.rearrange("(p t) i -> p (t i)", t=USER_TILES)

    with ExitStack() as ctx:
        consts = ctx.enter_context(tc.tile_pool(name="consts", bufs=1))
        rows = ctx.enter_context(tc.tile_pool(name="rows", bufs=N_GROUPS))
        stage = ctx.enter_context(tc.tile_pool(name="stage", bufs=3))
        thetas = ctx.enter_context(tc.tile_pool(name="thetas", bufs=6))
        results = ctx.enter_context(tc.tile_pool(name="results", bufs=N_GROUPS))
        flipped = ctx.enter_context(tc.psum_pool(name="flipped", bufs=4))
        products = ctx.enter_context(tc.psum_pool(name="products", bufs=4))
        ctx.enter_context(tc.manual_schedule())

        item_rows = consts.tile([P, ITEM_TILES * COORDS], BF16)
        nc.sync.dma_start(out=item_rows[:].rearrange("p (j d) -> p j d", j=ITEM_TILES), in_=items_in)
        user_rows = {}
        for g in range(N_GROUPS):
            user_rows[g] = rows.tile([P, GROUP * COORDS], BF16, name="user_rows")
            nc.sync.dma_start(
                out=user_rows[g][:], in_=users_in[:, g * GROUP * COORDS : (g + 1) * GROUP * COORDS]
            )

        identity = consts.tile([P, P], F32)
        make_identity(nc, identity[:])
        minus_one = consts.tile([P, 1], F32)
        nc.vector.memset(minus_one[:], -1.0)
        table_warmer = consts.tile([P, 1], F32)
        nc.scalar.activation(out=table_warmer[:], in_=minus_one[:], func=ACT.Sqrt, scale=-1.0)

        def transpose_tiles(source, n_tiles):
            words = source[:].bitcast(F32)
            banks = []
            for b in range(n_tiles // TILES_PER_BANK):
                bank = flipped.tile([P, TILES_PER_BANK, HALVES, P], F32, name="bank")
                for t in range(TILES_PER_BANK):
                    for u in range(HALVES):
                        first = ((b * TILES_PER_BANK + t) * HALVES + u) * P
                        nc.tensor.transpose(bank[:, t, u, :], words[:, first : first + P], identity[:])
                banks.append(bank)
            return banks

        def regroup(copy, bank, grouped, b):
            as_words = grouped[:].bitcast(F32).rearrange("p (t r u) -> p t r u", r=P, u=HALVES)
            copy(
                out=as_words[:, b * TILES_PER_BANK : (b + 1) * TILES_PER_BANK],
                in_=bank[:].rearrange("p t u r -> p t r u"),
            )

        def quantise(pool, grouped, n_tiles):
            codes = pool.tile([P, n_tiles * P], U32, name="codes%d" % n_tiles, align_bytes=64)
            scales = pool.tile([P, n_tiles * P], U8, name="scales%d" % n_tiles, align_bytes=64)
            nc.vector.quantize_mx(out=codes[:].bitcast(FP8X4), scales=scales[:], in_=grouped[:])
            return codes, scales

        first_coord = item_rows[:].rearrange("p (j d) -> p j d", j=ITEM_TILES)[:, :, 0:1]
        nc.vector.tensor_scalar(out=first_coord, in0=first_coord, scalar1=-1.0, scalar2=None, op0=ALU.mult)
        item_banks = transpose_tiles(item_rows, ITEM_TILES)
        item_grouped = consts.tile([P, ITEM_TILES * COORDS], BF16, align_bytes=64)
        regroup(nc.vector.tensor_copy, item_banks[0], item_grouped, 0)
        item_codes, item_scales = quantise(consts, item_grouped, ITEM_TILES)

        banks_of, grouped_of, quantised_of, product_of, theta_of, work_of = {}, {}, {}, {}, {}, {}

        def transpose_users(g):
            banks_of[g] = transpose_tiles(user_rows[g], GROUP)

        def regroup_users(g):
            grouped_of[g] = stage.tile([P, GROUP * COORDS], BF16, name="grouped", align_bytes=64)
            for b in range(BANKS_PER_GROUP):
                on_vector = (g * BANKS_PER_GROUP + b) % 4 == 3
                regroup(nc.vector.tensor_copy if on_vector else nc.scalar.copy, banks_of[g][b], grouped_of[g], b)

        def quantise_users(g):
            quantised_of[g] = quantise(stage, grouped_of[g], GROUP)

        def multiply(g):
            codes, scales = quantised_of[g]
            product_of[g] = []
            for b in range(BANKS_PER_GROUP):
                bank = products.tile([P, TILES_PER_BANK, ITEMS], F32, name="product")
                for t in range(TILES_PER_BANK):
                    cols = slice((b * TILES_PER_BANK + t) * P, (b * TILES_PER_BANK + t + 1) * P)
                    nc.tensor.matmul_mx(
                        out=bank[:, t, :],
                        lhsT=codes[:, cols].bitcast(FP8X4),
                        lhsT_scale=scales[:, cols],
                        rhs=item_codes[:].bitcast(FP8X4),
                        rhs_scale=item_scales[:],
                        start=True,
                        stop=True,
                    )
                product_of[g].append(bank)

        def clamp(g):
            theta_of[g] = thetas.tile([P, GROUP_COLS], F32, name="minus_theta")
            width = TILES_PER_BANK * ITEMS
            for b in range(BANKS_PER_GROUP):
                nc.vector.tensor_scalar(
                    out=theta_of[g][:, b * width : (b + 1) * width],
                    in0=product_of[g][b][:].rearrange("p t i -> p (t i)"),
                    scalar1=-THETA_MIN,
                    scalar2=-THETA_MAX,
                    op0=ALU.min,
                    op1=ALU.max,
                )

        def square(g):
            work_of[g] = results.tile([P, GROUP_COLS], F32, name="work")
            nc.scalar.activation(out=work_of[g][:], in_=theta_of[g][:], func=ACT.Square)

        def root(g):
            nc.scalar.activation(out=work_of[g][:], in_=work_of[g][:], func=ACT.Sqrt, bias=minus_one[:], scale=1.0)

        def add_theta(g):
            nc.vector.tensor_tensor(out=work_of[g][:], in0=work_of[g][:], in1=theta_of[g][:], op=ALU.subtract)

        def run(stage_fn, g):
            if 0 <= g < N_GROUPS:
                stage_fn(g)

        LAST_LAG = 7
        for step in range(N_GROUPS + LAST_LAG):
            run(transpose_users, step)
            run(quantise_users, step - 2)
            run(multiply, step - 2)
            run(clamp, step - 3)
            run(regroup_users, step - 1)
            run(square, step - 4)
            run(root, step - 5)
            run(add_theta, step - LAST_LAG)

        for g in range(N_GROUPS):
            nc.scalar.activation(out=work_of[g][:], in_=work_of[g][:], func=ACT.Ln)
            nc.vector.scalar_tensor_tensor(
                out=work_of[g][:], in0=work_of[g][:], scalar=-1.0, in1=work_of[g][:], op0=ALU.mult, op1=ALU.mult
            )
            nc.sync.dma_start(out=result_out[:, g * GROUP_COLS : (g + 1) * GROUP_COLS], in_=work_of[g][:])
